import numpy as np
import ml_dtypes


def mxq(x, axis, fmt="e4m3"):
    dtype, down = {"e4m3": (ml_dtypes.float8_e4m3fn, 7), "e5m2": (ml_dtypes.float8_e5m2, 14)}[fmt]
    v = np.moveaxis(np.asarray(x, np.float32).astype(ml_dtypes.bfloat16).astype(np.float64), axis, -1)
    blocks = v.reshape(v.shape[:-1] + (-1, 32))
    amax = np.abs(blocks).max(-1, keepdims=True)
    byte = np.maximum(np.where(amax > 0, np.frexp(amax)[1] - 1 + 127, 0) - down, 1)
    scale = np.exp2(byte - 127.0)
    codes = (blocks / scale).astype(np.float32).astype(dtype).astype(np.float64)
    return np.moveaxis((codes * scale).reshape(v.shape), -1, axis)


WIDE = False


def mx_kscale(k):
    if not WIDE:
        return np.ones(k)
    levels = np.array([20, -20, 10, -10, 0])
    a = np.random.permutation(np.resize(levels, k // 512 * 4)).reshape(k // 512, 4)
    idx = np.arange(k)
    return np.exp2(a[idx // 512, idx % 128 // 32])


BF16 = ml_dtypes.bfloat16


def bf(x):
    return np.asarray(x, np.float32).astype(BF16)


def f64(x):
    return np.asarray(x).astype(np.float64)


B, N, F = 8, 512, 512


def setup_inputs():
    s = mx_kscale(N)[:, None]
    regional_means = np.random.standard_normal((B, N, F)) * (4.0 / np.sqrt(N))
    adj = np.random.uniform(0.0, 1.0, (B, N, N)) * s
    g = np.random.standard_normal((B, N, F)) * np.exp2(np.random.randint(-12, 1, (B, N, 1))) / s
    return {"regional_means": bf(regional_means), "adj": bf(adj), "grad_out": bf(g)}


def reference(regional_means, adj, grad_out):
    n = adj.shape[-1]
    mask = 1.0 - np.eye(n)
    adj_masked = f64(adj) * mask
    aq = mxq(adj_masked, 1, "e4m3")
    gq = mxq(f64(grad_out), 1, "e5m2")
    return np.swapaxes(aq, 1, 2) @ gq

@@ -1,0 +1,166 @@
+from contextlib import ExitStack
+
+import concourse.masks as masks
+import concourse.mybir as mybir
+
+B, N, F = 8, 512, 512
+FLOPS = 2 * B * N * N * F
+BYTES = B * N * N * 2 + B * N * F * 2 + B * N * F * 4
+
+BF16 = mybir.dt.bfloat16
+F32 = mybir.dt.float32
+U32 = mybir.dt.uint32
+U8 = mybir.dt.uint8
+E4X4 = mybir.dt.float8_e4m3fn_x4
+E5X4 = mybir.dt.float8_e5m2_x4
+MULT = mybir.AluOpType.mult
+ADD = mybir.AluOpType.add
+
+P = 128
+PACK = 4
+U = 1
+E = PACK // U
+RAW_W = 640 * PACK
+V_COLS = 128
+LONG_ROWS = False
+PIN = True
+
+
+def planes(src):
+    return src[:, 0 : PACK * 512].rearrange("p (t w) -> p t w", t=PACK)
+
+
+def regroup(copy, dst, src, c0, c1):
+    copy(
+        out=dst[:, c0:c1, :].rearrange("p (c i) t -> p c t i", i=4),
+        in_=planes(src)[:, :, c0:c1].rearrange("p t (c i) -> p c t i", i=4),
+    )
+
+
+def regroup_by_residue(copy, dst, src):
+    copy(
+        out=dst[:].rearrange("p (m c) t -> p c t m", m=4),
+        in_=planes(src).rearrange("p t (c m) -> p c t m", m=4),
+    )
+
+
+def tile_gcn_t_kernel(tc, regional_means, adj, grad_out, out):
+    nc = tc.nc
+    with ExitStack() as ctx:
+        const = ctx.enter_context(tc.tile_pool(name="const", bufs=1))
+        raw = ctx.enter_context(tc.tile_pool(name="raw", bufs=1))
+        grp = ctx.enter_context(tc.tile_pool(name="grp", bufs=3))
+        mx = ctx.enter_context(tc.tile_pool(name="mx", bufs=3))
+        res = ctx.enter_context(tc.tile_pool(name="res", bufs=8))
+        psum = ctx.enter_context(tc.psum_pool(name="psum", bufs=8))
+        if PIN:
+            ctx.enter_context(tc.manual_schedule())
+
+        a_raw = []
+        g_raw = []
+        for b in range(B):
+            ar = raw.tile([P, RAW_W], BF16, name="a_raw%d" % b)
+            gr = raw.tile([P, PACK * 512], BF16, name="g_raw%d" % b)
+            nc.sync.dma_start(
+                out=ar[:, 0 : PACK * 512].rearrange("p (u x) -> p u x", u=U),
+                in_=adj[b].rearrange("(u p e) w -> p u (e w)", u=U, e=E),
+            )
+            nc.sync.dma_start(
+                out=gr[:].rearrange("p (u x) -> p u x", u=U),
+                in_=grad_out[b].rearrange("(u p e) w -> p u (e w)", u=U, e=E),
+            )
+            a_raw.append(ar)
+            g_raw.append(gr)
+
+        mk = const.tile([P, E, P * E], BF16, name="mk")
+        nc.vector.memset(mk[:], 1.0)
+        ident = const.tile([P, P], BF16, name="ident")
+        masks.make_identity(nc, ident[:])
+        inot = const.tile([P, P], BF16, name="inot")
+        nc.vector.tensor_scalar(out=inot[:], in0=ident[:], scalar1=-1.0, scalar2=1.0, op0=MULT, op1=ADD)
+        for e in range(E):
+            nc.vector.tensor_copy(out=mk[:].rearrange("p e (q f) -> p e q f", f=E)[:, e, :, e], in_=inot[:])
+
+        a_grp = {}
+        g_grp = {}
+        a_mx = {}
+        g_mx = {}
+
+        def mask(b):
+            win = (
+                a_raw[b][:]
+                .rearrange("p (u y) -> p u y", u=U)[:, :, 0 : 512 * E]
+                .rearrange("p u (e w) -> p u e w", e=E)[:, :, :, 0 : P * E]
+            )
+            nc.vector.tensor_tensor(
+                out=win, in0=win, in1=mk[:].unsqueeze(1).to_broadcast([P, U, E, P * E]), op=MULT
+            )
+
+        def reg_a(b):
+            a_grp[b] = grp.tile([P, 512, PACK], BF16, name="a_grp", align_bytes=64)
+            if LONG_ROWS:
+                regroup_by_residue(nc.vector.tensor_copy, a_grp[b], a_raw[b])
+            else:
+                regroup(nc.vector.tensor_copy, a_grp[b], a_raw[b], 0, 512)
+
+        def reg_g_scalar(b):
+            g_grp[b] = grp.tile([P, 512, PACK], BF16, name="g_grp", align_bytes=64)
+            regroup(nc.scalar.copy, g_grp[b], g_raw[b], V_COLS, 512)
+
+        def reg_g_vector(b):
+            regroup(nc.vector.tensor_copy, g_grp[b], g_raw[b], 0, V_COLS)
+
+        def quant(b, grouped, store, fmt, label):
+            codes = mx.tile([P, 512], U32, name=label + "_codes", align_bytes=64)
+            scl = mx.tile([P, 512], U8, name=label + "_scl", align_bytes=64)
+            nc.vector.quantize_mx(
+                out=codes[:].bitcast(fmt), scales=scl[:], in_=grouped[b][:].rearrange("p w t -> p (w t)")
+            )
+            store[b] = (codes, scl)
+
+        if LONG_ROWS:
+            out_view = [out[b].rearrange("(p m) f -> p m f", m=4) for b in range(B)]
+        else:
+            out_view = [out[b].rearrange("(m p) f -> p m f", p=P) for b in range(B)]
+
+        def product(b):
+            last = b == B - 1
+            a_codes, a_scl = a_mx[b]
+            g_codes, g_scl = g_mx[b]
+            o_sb = res.tile([P, 4, 512], F32, name="o_sb")
+            for m in range(4):
+                acc = psum.tile([P, 512], F32, name="acc")
+                nc.tensor.matmul_mx(
+                    out=acc[:],
+                    lhsT=a_codes[:, m * P : (m + 1) * P].bitcast(E4X4),
+                    lhsT_scale=a_scl[:, m * P : (m + 1) * P],
+                    rhs=g_codes[:].bitcast(E5X4),
+                    rhs_scale=g_scl[:],
+                    start=True,
+                    stop=True,
+                )
+                if last and m % 2 == 1:
+                    nc.vector.tensor_copy(out=o_sb[:, m, :], in_=acc[:])
+                else:
+                    nc.scalar.copy(out=o_sb[:, m, :], in_=acc[:])
+                if last and not LONG_ROWS:
+                    nc.sync.dma_start(out=out_view[b][:, m, :], in_=o_sb[:, m, :])
+            if LONG_ROWS or not last:
+                nc.sync.dma_start(out=out_view[b], in_=o_sb[:])
+
+        mask(0)
+        reg_g_scalar(0)
+        reg_a(0)
+        reg_g_vector(0)
+        for s in range(B):
+            more = s + 1 < B
+            if more:
+                mask(s + 1)
+                reg_g_scalar(s + 1)
+            quant(s, a_grp, a_mx, E4X4, "a")
+            if more:
+                reg_a(s + 1)
+            quant(s, g_grp, g_mx, E5X4, "g")
+            if more:
+                reg_g_vector(s + 1)
+            product(s)

@@ -22,7 +22,7 @@ U = 1
 E = PACK // U
 RAW_W = 640 * PACK
 V_COLS = 128
-LONG_ROWS = False
+LONG_ROWS = True
 PIN = True
 
 

@@ -18,10 +18,10 @@ ADD = mybir.AluOpType.add
 
 P = 128
 PACK = 4
-U = 1
+U = 4
 E = PACK // U
 RAW_W = 640 * PACK
-V_COLS = 128
+V_COLS = 256
 LONG_ROWS = True
 PIN = True
 

@@ -18,10 +18,10 @@ ADD = mybir.AluOpType.add
 
 P = 128
 PACK = 4
-U = 4
+U = 2
 E = PACK // U
 RAW_W = 640 * PACK
-V_COLS = 256
+V_COLS = 224
 LONG_ROWS = True
 PIN = True
 
@@ -143,9 +143,9 @@ def tile_gcn_t_kernel(tc, regional_means, adj, grad_out, out):
                     nc.vector.tensor_copy(out=o_sb[:, m, :], in_=acc[:])
                 else:
                     nc.scalar.copy(out=o_sb[:, m, :], in_=acc[:])
-                if last and not LONG_ROWS:
+                if last:
                     nc.sync.dma_start(out=out_view[b][:, m, :], in_=o_sb[:, m, :])
-            if LONG_ROWS or not last:
+            if not last:
                 nc.sync.dma_start(out=out_view[b], in_=o_sb[:])
 
         mask(0)

@@ -21,7 +21,7 @@ PACK = 4
 U = 2
 E = PACK // U
 RAW_W = 640 * PACK
-V_COLS = 224
+V_COLS = 256
 LONG_ROWS = True
 PIN = True
 

@@ -21,7 +21,7 @@ PACK = 4
 U = 2
 E = PACK // U
 RAW_W = 640 * PACK
-V_COLS = 256
+V_COLS = 192
 LONG_ROWS = True
 PIN = True
 

@@ -21,9 +21,10 @@ PACK = 4
 U = 2
 E = PACK // U
 RAW_W = 640 * PACK
-V_COLS = 192
+V_COLS = 224
 LONG_ROWS = True
 PIN = True
+LOADS = [(0, 1), (1, 1), (2, 2), (4, 2), (6, 2)]
 
 
 def planes(src):
@@ -58,19 +59,20 @@ def tile_gcn_t_kernel(tc, regional_means, adj, grad_out, out):
 
         a_raw = []
         g_raw = []
-        for b in range(B):
-            ar = raw.tile([P, RAW_W], BF16, name="a_raw%d" % b)
-            gr = raw.tile([P, PACK * 512], BF16, name="g_raw%d" % b)
+        for first, count in LOADS:
+            ar = raw.tile([P, (count - 1) * PACK * 512 + RAW_W], BF16, name="a_raw%d" % first)
+            gr = raw.tile([P, count * PACK * 512], BF16, name="g_raw%d" % first)
             nc.sync.dma_start(
-                out=ar[:, 0 : PACK * 512].rearrange("p (u x) -> p u x", u=U),
-                in_=adj[b].rearrange("(u p e) w -> p u (e w)", u=U, e=E),
+                out=ar[:, 0 : count * PACK * 512].rearrange("p (v x) -> p v x", v=count * U),
+                in_=adj[first : first + count].rearrange("b (u p e) w -> p (b u) (e w)", u=U, e=E),
             )
             nc.sync.dma_start(
-                out=gr[:].rearrange("p (u x) -> p u x", u=U),
-                in_=grad_out[b].rearrange("(u p e) w -> p u (e w)", u=U, e=E),
+                out=gr[:].rearrange("p (v x) -> p v x", v=count * U),
+                in_=grad_out[first : first + count].rearrange("b (u p e) w -> p (b u) (e w)", u=U, e=E),
             )
-            a_raw.append(ar)
-            g_raw.append(gr)
+            for k in range(count):
+                a_raw.append(ar[:, k * PACK * 512 : k * PACK * 512 + RAW_W])
+                g_raw.append(gr[:, k * PACK * 512 : (k + 1) * PACK * 512])
 
         mk = const.tile([P, E, P * E], BF16, name="mk")
         nc.vector.memset(mk[:], 1.0)

@@ -147,8 +147,8 @@ def tile_gcn_t_kernel(tc, regional_means, adj, grad_out, out):
                     nc.scalar.copy(out=o_sb[:, m, :], in_=acc[:])
                 if last:
                     nc.sync.dma_start(out=out_view[b][:, m, :], in_=o_sb[:, m, :])
-            if not last:
-                nc.sync.dma_start(out=out_view[b], in_=o_sb[:])
+                elif m % 2 == 1:
+                    nc.sync.dma_start(out=out_view[b][:, m - 1 : m + 1, :], in_=o_sb[:, m - 1 : m + 1, :])
 
         mask(0)
         reg_g_scalar(0)

@@ -24,6 +24,7 @@ RAW_W = 640 * PACK
 V_COLS = 224
 LONG_ROWS = True
 PIN = True
+HALF_FROM = 5
 LOADS = [(0, 1), (1, 1), (2, 2), (4, 2), (6, 2)]
 
 
@@ -147,8 +148,10 @@ def tile_gcn_t_kernel(tc, regional_means, adj, grad_out, out):
                     nc.scalar.copy(out=o_sb[:, m, :], in_=acc[:])
                 if last:
                     nc.sync.dma_start(out=out_view[b][:, m, :], in_=o_sb[:, m, :])
-                elif m % 2 == 1:
+                elif b >= HALF_FROM and m % 2 == 1:
                     nc.sync.dma_start(out=out_view[b][:, m - 1 : m + 1, :], in_=o_sb[:, m - 1 : m + 1, :])
+            if b < HALF_FROM:
+                nc.sync.dma_start(out=out_view[b], in_=o_sb[:])
 
         mask(0)
         reg_g_scalar(0)

from contextlib import ExitStack

import concourse.masks as masks
import concourse.mybir as mybir

B, N, F = 8, 512, 512
FLOPS = 2 * B * N * N * F
BYTES = B * N * N * 2 + B * N * F * 2 + B * N * F * 4

BF16 = mybir.dt.bfloat16
F32 = mybir.dt.float32
U32 = mybir.dt.uint32
U8 = mybir.dt.uint8
E4X4 = mybir.dt.float8_e4m3fn_x4
E5X4 = mybir.dt.float8_e5m2_x4
MULT = mybir.AluOpType.mult
ADD = mybir.AluOpType.add

P = 128
PACK = 4
U = 2
E = PACK // U
RAW_W = 640 * PACK
V_COLS = 224
LONG_ROWS = True
PIN = True
HALF_FROM = 5
LOADS = [(0, 1), (1, 1), (2, 2), (4, 2), (6, 2)]


def planes(src):
    return src[:, 0 : PACK * 512].rearrange("p (t w) -> p t w", t=PACK)


def regroup(copy, dst, src, c0, c1):
    copy(
        out=dst[:, c0:c1, :].rearrange("p (c i) t -> p c t i", i=4),
        in_=planes(src)[:, :, c0:c1].rearrange("p t (c i) -> p c t i", i=4),
    )


def regroup_by_residue(copy, dst, src):
    copy(
        out=dst[:].rearrange("p (m c) t -> p c t m", m=4),
        in_=planes(src).rearrange("p t (c m) -> p c t m", m=4),
    )


def tile_gcn_t_kernel(tc, regional_means, adj, grad_out, out):
    nc = tc.nc
    with ExitStack() as ctx:
        const = ctx.enter_context(tc.tile_pool(name="const", bufs=1))
        raw = ctx.enter_context(tc.tile_pool(name="raw", bufs=1))
        grp = ctx.enter_context(tc.tile_pool(name="grp", bufs=3))
        mx = ctx.enter_context(tc.tile_pool(name="mx", bufs=3))
        res = ctx.enter_context(tc.tile_pool(name="res", bufs=8))
        psum = ctx.enter_context(tc.psum_pool(name="psum", bufs=8))
        if PIN:
            ctx.enter_context(tc.manual_schedule())

        a_raw = []
        g_raw = []
        for first, count in LOADS:
            ar = raw.tile([P, (count - 1) * PACK * 512 + RAW_W], BF16, name="a_raw%d" % first)
            gr = raw.tile([P, count * PACK * 512], BF16, name="g_raw%d" % first)
            nc.sync.dma_start(
                out=ar[:, 0 : count * PACK * 512].rearrange("p (v x) -> p v x", v=count * U),
                in_=adj[first : first + count].rearrange("b (u p e) w -> p (b u) (e w)", u=U, e=E),
            )
            nc.sync.dma_start(
                out=gr[:].rearrange("p (v x) -> p v x", v=count * U),
                in_=grad_out[first : first + count].rearrange("b (u p e) w -> p (b u) (e w)", u=U, e=E),
            )
            for k in range(count):
                a_raw.append(ar[:, k * PACK * 512 : k * PACK * 512 + RAW_W])
                g_raw.append(gr[:, k * PACK * 512 : (k + 1) * PACK * 512])

        mk = const.tile([P, E, P * E], BF16, name="mk")
        nc.vector.memset(mk[:], 1.0)
        ident = const.tile([P, P], BF16, name="ident")
        masks.make_identity(nc, ident[:])
        inot = const.tile([P, P], BF16, name="inot")
        nc.vector.tensor_scalar(out=inot[:], in0=ident[:], scalar1=-1.0, scalar2=1.0, op0=MULT, op1=ADD)
        for e in range(E):
            nc.vector.tensor_copy(out=mk[:].rearrange("p e (q f) -> p e q f", f=E)[:, e, :, e], in_=inot[:])

        a_grp = {}
        g_grp = {}
        a_mx = {}
        g_mx = {}

        def mask(b):
            win = (
                a_raw[b][:]
                .rearrange("p (u y) -> p u y", u=U)[:, :, 0 : 512 * E]
                .rearrange("p u (e w) -> p u e w", e=E)[:, :, :, 0 : P * E]
            )
            nc.vector.tensor_tensor(
                out=win, in0=win, in1=mk[:].unsqueeze(1).to_broadcast([P, U, E, P * E]), op=MULT
            )

        def reg_a(b):
            a_grp[b] = grp.tile([P, 512, PACK], BF16, name="a_grp", align_bytes=64)
            if LONG_ROWS:
                regroup_by_residue(nc.vector.tensor_copy, a_grp[b], a_raw[b])
            else:
                regroup(nc.vector.tensor_copy, a_grp[b], a_raw[b], 0, 512)

        def reg_g_scalar(b):
            g_grp[b] = grp.tile([P, 512, PACK], BF16, name="g_grp", align_bytes=64)
            regroup(nc.scalar.copy, g_grp[b], g_raw[b], V_COLS, 512)

        def reg_g_vector(b):
            regroup(nc.vector.tensor_copy, g_grp[b], g_raw[b], 0, V_COLS)

        def quant(b, grouped, store, fmt, label):
            codes = mx.tile([P, 512], U32, name=label + "_codes", align_bytes=64)
            scl = mx.tile([P, 512], U8, name=label + "_scl", align_bytes=64)
            nc.vector.quantize_mx(
                out=codes[:].bitcast(fmt), scales=scl[:], in_=grouped[b][:].rearrange("p w t -> p (w t)")
            )
            store[b] = (codes, scl)

        if LONG_ROWS:
            out_view = [out[b].rearrange("(p m) f -> p m f", m=4) for b in range(B)]
        else:
            out_view = [out[b].rearrange("(m p) f -> p m f", p=P) for b in range(B)]

        def product(b):
            last = b == B - 1
            a_codes, a_scl = a_mx[b]
            g_codes, g_scl = g_mx[b]
            o_sb = res.tile([P, 4, 512], F32, name="o_sb")
            for m in range(4):
                acc = psum.tile([P, 512], F32, name="acc")
                nc.tensor.matmul_mx(
                    out=acc[:],
                    lhsT=a_codes[:, m * P : (m + 1) * P].bitcast(E4X4),
                    lhsT_scale=a_scl[:, m * P : (m + 1) * P],
                    rhs=g_codes[:].bitcast(E5X4),
                    rhs_scale=g_scl[:],
                    start=True,
                    stop=True,
                )
                if last and m % 2 == 1:
                    nc.vector.tensor_copy(out=o_sb[:, m, :], in_=acc[:])
                else:
                    nc.scalar.copy(out=o_sb[:, m, :], in_=acc[:])
                if last:
                    nc.sync.dma_start(out=out_view[b][:, m, :], in_=o_sb[:, m, :])
                elif b >= HALF_FROM and m % 2 == 1:
                    nc.sync.dma_start(out=out_view[b][:, m - 1 : m + 1, :], in_=o_sb[:, m - 1 : m + 1, :])
            if b < HALF_FROM:
                nc.sync.dma_start(out=out_view[b], in_=o_sb[:])

        mask(0)
        reg_g_scalar(0)
        reg_a(0)
        reg_g_vector(0)
        for s in range(B):
            more = s + 1 < B
            if more:
                mask(s + 1)
                reg_g_scalar(s + 1)
            quant(s, a_grp, a_mx, E4X4, "a")
            if more:
                reg_a(s + 1)
            quant(s, g_grp, g_mx, E5X4, "g")
            if more:
                reg_g_vector(s + 1)
            product(s)
